import numpy as np
import ml_dtypes


def mxq(x, axis, fmt="e4m3"):
    dtype, down = {"e4m3": (ml_dtypes.float8_e4m3fn, 7), "e5m2": (ml_dtypes.float8_e5m2, 14)}[fmt]
    v = np.moveaxis(np.asarray(x, np.float32).astype(ml_dtypes.bfloat16).astype(np.float64), axis, -1)
    blocks = v.reshape(v.shape[:-1] + (-1, 32))
    amax = np.abs(blocks).max(-1, keepdims=True)
    byte = np.maximum(np.where(amax > 0, np.frexp(amax)[1] - 1 + 127, 0) - down, 1)
    scale = np.exp2(byte - 127.0)
    codes = (blocks / scale).astype(np.float32).astype(dtype).astype(np.float64)
    return np.moveaxis((codes * scale).reshape(v.shape), -1, axis)


WIDE = False


def mx_kscale(k):
    if not WIDE:
        return np.ones(k)
    levels = np.array([10, -10, 5, -5, 0])
    a = np.random.permutation(np.resize(levels, k // 512 * 4)).reshape(k // 512, 4)
    idx = np.arange(k)
    return np.exp2(a[idx // 512, idx % 128 // 32])


BF16 = ml_dtypes.bfloat16


def bf(x):
    return np.asarray(x, np.float32).astype(BF16)


def f64(x):
    return np.asarray(x).astype(np.float64)


E2M1 = np.array([0.0, 0.5, 1.0, 1.5, 2.0, 3.0, 4.0, 6.0, -0.0, -0.5, -1.0, -1.5, -2.0, -3.0, -4.0, -6.0])


def pack_weight(w, fmt):
    k, n = w.shape
    w = f64(bf(w)).reshape(k // 32, 32, n)
    amax = np.abs(w).max(1)
    if fmt == "e4m3":
        byte = np.frexp(amax)[1] - 1 + 127 - 7
    else:
        mant, ex = np.frexp(amax / 6.0)
        byte = np.where(mant > 0.5, ex, ex - 1) + 127
    byte = np.clip(np.where(amax > 0, byte, 1), 1, 254)
    scaled = (w * np.exp2(127.0 - byte)[:, None, :]).reshape(k, n).astype(np.float32)
    by_word = np.ascontiguousarray(scaled.reshape(k // 512, 128, 4, n).transpose(0, 1, 3, 2))
    if fmt == "e4m3":
        words = by_word.astype(ml_dtypes.float8_e4m3fn).view(np.uint8)
    else:
        c = by_word.astype(ml_dtypes.float4_e2m1fn).view(np.uint8) & 0xF
        words = c[..., 0::2] | (c[..., 1::2] << 4)
    return np.ascontiguousarray(words), np.ascontiguousarray(byte.astype(np.uint8).reshape(k // 512, 16, n))


def unpack_weight(words, scales, fmt):
    g, p, n, _ = words.shape
    if fmt == "e4m3":
        vals = np.ascontiguousarray(words).view(ml_dtypes.float8_e4m3fn).astype(np.float64)
    else:
        nib = np.empty((g, p, n, 4), np.uint8)
        nib[..., 0::2] = words & 0xF
        nib[..., 1::2] = words >> 4
        vals = E2M1[nib]
    vals = vals * np.repeat(np.exp2(scales.astype(np.float64) - 127.0), 8, axis=1)[..., None]
    return vals.transpose(0, 1, 3, 2).reshape(g * 512, n)


B, S, DV, D, H, A = 2, 256, 1024, 1024, 8, 64
LN_EPS = 1e-3


def setup_inputs():
    s = mx_kscale(DV)
    attn = bf(np.random.standard_normal((B, H, S, DV)) * 0.4 * s)
    Wo = np.random.standard_normal((H, DV, D)) * 0.6 / np.sqrt(DV * H) / s[None, :, None]
    Wo_words, Wo_scales = pack_weight(Wo.reshape(-1, D), "e4m3")
    return {
        "attn": attn,
        "Wo_words": Wo_words,
        "Wo_scales": Wo_scales,
        "bo": bf(np.random.standard_normal((H, D)) * 0.12 / np.sqrt(H)),
        "query_inputs": bf(np.random.standard_normal((B, S, D)) * 0.1),
        "gamma": bf(1.0 + 0.1 * np.random.standard_normal(D)),
        "beta": bf(0.1 * np.random.standard_normal(D)),
    }


def reference(attn, Wo_words, Wo_scales, bo, query_inputs, gamma, beta):
    pre = mxq(f64(attn), 3, "e4m3") @ unpack_weight(Wo_words, Wo_scales, "e4m3").reshape(H, DV, D)
    head_out = np.maximum(pre + f64(bo)[None, :, None, :], 0.0)
    x = f64(query_inputs) + head_out.sum(axis=1)
    mean = x.mean(axis=-1, keepdims=True)
    var = x.var(axis=-1, keepdims=True)
    return f64(gamma) * (x - mean) / np.sqrt(var + LN_EPS) + f64(beta)

@@ -1,0 +1,256 @@
+from contextlib import ExitStack
+
+import concourse.mybir as mybir
+from concourse.masks import make_identity
+
+F32 = mybir.dt.float32
+BF16 = mybir.dt.bfloat16
+I32 = mybir.dt.int32
+U32 = mybir.dt.uint32
+U8 = mybir.dt.uint8
+FP8X4 = mybir.dt.float8_e4m3fn_x4
+ALU = mybir.AluOpType
+ACT = mybir.ActivationFunctionType
+
+B, H, S, DV, D = 2, 8, 256, 1024, 1024
+LN_EPS = 1e-3
+FLOPS = 2 * B * H * S * DV * D
+
+P = 128
+K_PASS = 4 * P
+GROUPS = DV // K_PASS
+WORDS = K_PASS // 2
+D_TILES = D // P
+TOKEN_TILES = S // P
+PAIR = 2
+PAIRS = H // PAIR
+BANK = 512
+PLANES = 4
+PLANE_SETS = H * GROUPS // PLANES
+
+
+def tile_multiheadattentionunit_pa_e_kernel(
+    tc, attn, Wo_words, Wo_scales, bo, query_inputs, gamma, beta, out
+):
+    nc = tc.nc
+    with ExitStack() as ctx:
+        keep = ctx.enter_context(tc.tile_pool(name="keep", bufs=1))
+        stage = ctx.enter_context(tc.tile_pool(name="stage", bufs=2))
+        terms = ctx.enter_context(tc.tile_pool(name="terms", bufs=4))
+        small = ctx.enter_context(tc.tile_pool(name="small", bufs=4))
+        psum_t = ctx.enter_context(tc.psum_pool(name="psum_t", bufs=4))
+        psum_mx = ctx.enter_context(tc.psum_pool(name="psum_mx", bufs=4))
+
+        ident = keep.tile([P, P], F32)
+        make_identity(nc, ident[:])
+
+        eps = keep.tile([P, 1], F32)
+        nc.vector.memset(eps[:], LN_EPS)
+        warm = keep.tile([P, 1], F32)
+        nc.scalar.activation(out=warm[:], in_=eps[:], func=ACT.Sqrt)
+
+        a_raw = {}
+
+        def load_attn(b, pair):
+            a_raw[b, pair] = keep.tile([P, PAIR, TOKEN_TILES, DV], BF16, name="a_raw%d_%d" % (b, pair))
+            for i in range(PAIR):
+                nc.sync.dma_start(
+                    out=a_raw[b, pair][:, i],
+                    in_=attn[b, PAIR * pair + i].rearrange("(p r) k -> p r k", r=TOKEN_TILES),
+                )
+
+        w_words = {}
+
+        def load_weight(h):
+            w_words[h] = keep.tile([P, GROUPS, D], U32, name="w_words%d" % h, align_bytes=64)
+            nc.sync.dma_start(
+                out=w_words[h][:].bitcast(I32),
+                in_=Wo_words[GROUPS * h : GROUPS * (h + 1)].rearrange("g p n t -> p g (n t)").bitcast(I32),
+            )
+
+        load_attn(0, 0)
+
+        b_rows = keep.tile([P, P], BF16)
+        nc.vector.memset(b_rows[:], 0.0)
+        nc.scalar.dma_start(out=b_rows[0 : H * D_TILES, :], in_=bo.rearrange("h (t p) -> (h t) p", p=P))
+
+        w_planes = keep.tile([P, PLANE_SETS, D], U8, align_bytes=64)
+        nc.vector.memset(w_planes[:].bitcast(I32), 0)
+        for j in range(PLANE_SETS):
+            for quadrant in range(4):
+                nc.sync.dma_start(
+                    out=w_planes[32 * quadrant : 32 * quadrant + 4 * PLANES, j, :].bitcast(I32),
+                    in_=Wo_scales[PLANES * j : PLANES * (j + 1), 4 * quadrant : 4 * quadrant + 4, :].bitcast(I32),
+                )
+
+        for pair in range(PAIRS):
+            if pair > 0:
+                load_attn(0, pair)
+            for i in range(PAIR):
+                load_weight(PAIR * pair + i)
+
+        q_sb = {}
+        gamma_b = keep.tile([P, D], BF16)
+        beta_b = keep.tile([P, D], BF16)
+        for b in range(B):
+            q_sb[b] = keep.tile([P, TOKEN_TILES, D], BF16, name="q_sb%d" % b)
+        load_attn(1, 0)
+        nc.sync.dma_start(out=q_sb[0][:], in_=query_inputs[0].rearrange("(p r) d -> p r d", r=TOKEN_TILES))
+        nc.sync.dma_start(out=gamma_b[:], in_=gamma.partition_broadcast(P))
+        nc.sync.dma_start(out=beta_b[:], in_=beta.partition_broadcast(P))
+        for pair in range(1, PAIRS):
+            load_attn(1, pair)
+        nc.sync.dma_start(out=q_sb[1][:], in_=query_inputs[1].rearrange("(p r) d -> p r d", r=TOKEN_TILES))
+
+        b_rows32 = keep.tile([P, P], F32)
+        nc.vector.tensor_copy(out=b_rows32[:], in_=b_rows[:])
+        b_cols = psum_t.tile([P, P], F32, tag="t")
+        nc.tensor.transpose(b_cols[:], b_rows32[:], ident[:])
+        bias = keep.tile([P, H, D_TILES], F32)
+        neg_bias = keep.tile([P, H, D_TILES], F32)
+        bias_sum = keep.tile([P, D_TILES], F32)
+        nc.vector.tensor_copy(out=bias[:].rearrange("p h t -> p (h t)"), in_=b_cols[:, 0 : H * D_TILES])
+        nc.vector.tensor_scalar(
+            out=neg_bias[:].rearrange("p h t -> p (h t)"),
+            in0=b_cols[:, 0 : H * D_TILES],
+            scalar1=-1.0,
+            scalar2=None,
+            op0=ALU.mult,
+        )
+        nc.vector.tensor_reduce(
+            out=bias_sum[:], in_=bias[:].rearrange("p h t -> p t h"), axis=mybir.AxisListType.X, op=ALU.add
+        )
+
+        a_codes = {}
+        a_scales = {}
+        head_sum = {}
+        for b in range(B):
+            head_sum[b] = keep.tile([P, D_TILES, S], F32, name="head_sum%d" % b)
+
+        def quantise_pair(b, pair):
+            grouped = stage.tile([P, PAIR, GROUPS, S, 4], BF16, align_bytes=64)
+            a_codes[b, pair] = stage.tile([P, PAIR, GROUPS, S], U32, name="a_codes", align_bytes=64)
+            a_scales[b, pair] = stage.tile([P, PAIR, GROUPS, S], U8, name="a_scales", align_bytes=64)
+            for i in range(PAIR):
+                for g in range(GROUPS):
+                    pairs_t = psum_t.tile([P, 2, S], F32, tag="t")
+                    for u in range(2):
+                        for r in range(TOKEN_TILES):
+                            words = a_raw[b, pair][:, i, r, :].bitcast(F32)
+                            nc.tensor.transpose(
+                                pairs_t[:, u, P * r : P * (r + 1)],
+                                words[:, WORDS * g + u : WORDS * (g + 1) : 2],
+                                ident[:],
+                            )
+                    nc.scalar.copy(
+                        out=grouped[:, i, g].rearrange("p n t -> p (n t)").bitcast(F32).rearrange("p (n u) -> p n u", u=2),
+                        in_=pairs_t[:].rearrange("p u n -> p n u"),
+                    )
+            for i in range(PAIR):
+                nc.vector.quantize_mx(
+                    out=a_codes[b, pair][:, i].rearrange("p g n -> p (g n)").bitcast(FP8X4),
+                    scales=a_scales[b, pair][:, i].rearrange("p g n -> p (g n)"),
+                    in_=grouped[:, i].rearrange("p g n t -> p (g n t)"),
+                )
+
+        def leave_psum(b, h, t, product):
+            total = head_sum[b][:, t, :]
+            if t % 3 == 1:
+                if h == 0:
+                    nc.scalar.activation(out=total, in_=product, func=ACT.Relu, bias=bias[:, h, t : t + 1])
+                else:
+                    term = terms.tile([P, S], F32)
+                    nc.scalar.activation(out=term[:], in_=product, func=ACT.Relu, bias=bias[:, h, t : t + 1])
+                    nc.gpsimd.tensor_tensor(out=total, in0=total, in1=term[:], op=ALU.add)
+            elif h == 0:
+                nc.vector.tensor_scalar(
+                    out=total,
+                    in0=product,
+                    scalar1=neg_bias[:, h, t : t + 1],
+                    scalar2=bias_sum[:, t : t + 1],
+                    op0=ALU.max,
+                    op1=ALU.add,
+                )
+            else:
+                nc.vector.scalar_tensor_tensor(
+                    out=total,
+                    in0=product,
+                    scalar=neg_bias[:, h, t : t + 1],
+                    in1=total,
+                    op0=ALU.max,
+                    op1=ALU.add,
+                )
+
+        def multiply_pair(b, pair):
+            for i in range(PAIR):
+                h = PAIR * pair + i
+                for t in range(D_TILES):
+                    product = psum_mx.tile([P, S], F32)
+                    for g in range(GROUPS):
+                        plane_set, plane = divmod(GROUPS * h + g, PLANES)
+                        nc.tensor.matmul_mx(
+                            out=product[:],
+                            lhsT=w_words[h][:, g, P * t : P * (t + 1)].bitcast(FP8X4),
+                            lhsT_scale=w_planes[4 * plane : P, plane_set, P * t : P * (t + 1)],
+                            rhs=a_codes[b, pair][:, i, g, :].bitcast(FP8X4),
+                            rhs_scale=a_scales[b, pair][:, i, g, :],
+                            start=(g == 0),
+                            stop=(g == GROUPS - 1),
+                        )
+                    leave_psum(b, h, t, product[:])
+
+        def layer_norm(b, r):
+            x = stage.tile([P, D], F32)
+            half_sums = small.tile([P, D // BANK], F32)
+            for c in range(D // BANK):
+                x_t = psum_t.tile([P, BANK], F32, tag="t")
+                for j in range(BANK // P):
+                    nc.tensor.transpose(
+                        x_t[:, P * j : P * (j + 1)],
+                        head_sum[b][:, (BANK // P) * c + j, P * r : P * (r + 1)],
+                        ident[:],
+                    )
+                nc.vector.scalar_tensor_tensor(
+                    out=x[:, BANK * c : BANK * (c + 1)],
+                    in0=x_t[:],
+                    scalar=1.0,
+                    in1=q_sb[b][:, r, BANK * c : BANK * (c + 1)],
+                    op0=ALU.mult,
+                    op1=ALU.add,
+                    accum_out=half_sums[:, c : c + 1],
+                )
+            neg_mean = small.tile([P, 1], F32)
+            nc.vector.tensor_scalar(
+                out=neg_mean[:],
+                in0=half_sums[:, 0:1],
+                scalar1=half_sums[:, 1:2],
+                scalar2=-1.0 / D,
+                op0=ALU.add,
+                op1=ALU.mult,
+            )
+            squares = stage.tile([P, D], BF16)
+            sum_sq = small.tile([P, 1], F32)
+            nc.scalar.activation(out=squares[:], in_=x[:], func=ACT.Square, bias=neg_mean[:], accum_out=sum_sq[:])
+            y = stage.tile([P, D], F32)
+            nc.vector.scalar_tensor_tensor(
+                out=y[:], in0=x[:], scalar=neg_mean[:], in1=gamma_b[:], op0=ALU.add, op1=ALU.mult
+            )
+            std = small.tile([P, 1], F32)
+            nc.scalar.activation(out=std[:], in_=sum_sq[:], func=ACT.Sqrt, bias=eps[:], scale=1.0 / D)
+            rstd = small.tile([P, 1], F32)
+            nc.vector.reciprocal(out=rstd[:], in_=std[:])
+            nc.vector.scalar_tensor_tensor(
+                out=y[:], in0=y[:], scalar=rstd[:], in1=beta_b[:], op0=ALU.mult, op1=ALU.add
+            )
+            nc.sync.dma_start(out=out[b].rearrange("(p r) d -> p r d", r=TOKEN_TILES)[:, r, :], in_=y[:])
+
+        steps = [(b, pair) for b in range(B) for pair in range(PAIRS)]
+        quantise_pair(*steps[0])
+        for n, (b, pair) in enumerate(steps):
+            if n + 1 < len(steps):
+                quantise_pair(*steps[n + 1])
+            multiply_pair(b, pair)
+            if b > 0 and pair < TOKEN_TILES:
+                layer_norm(b - 1, pair)
+        for r in range(TOKEN_TILES):
+            layer_norm(B - 1, r)

@@ -25,6 +25,7 @@ TOKEN_TILES = S // P
 PAIR = 2
 PAIRS = H // PAIR
 BANK = 512
+PER_BANK = BANK // S
 PLANES = 4
 PLANE_SETS = H * GROUPS // PLANES
 
@@ -34,6 +35,7 @@ def tile_multiheadattentionunit_pa_e_kernel(
 ):
     nc = tc.nc
     with ExitStack() as ctx:
+        ctx.enter_context(tc.manual_schedule())
         keep = ctx.enter_context(tc.tile_pool(name="keep", bufs=1))
         stage = ctx.enter_context(tc.tile_pool(name="stage", bufs=2))
         terms = ctx.enter_context(tc.tile_pool(name="terms", bufs=4))
@@ -44,11 +46,16 @@ def tile_multiheadattentionunit_pa_e_kernel(
         ident = keep.tile([P, P], F32)
         make_identity(nc, ident[:])
 
-        eps = keep.tile([P, 1], F32)
-        nc.vector.memset(eps[:], LN_EPS)
-        warm = keep.tile([P, 1], F32)
-        nc.scalar.activation(out=warm[:], in_=eps[:], func=ACT.Sqrt)
+        b_rows = keep.tile([P, P], BF16)
+        nc.sync.dma_start(out=b_rows[0 : H * D_TILES, :], in_=bo.rearrange("h (t p) -> (h t) p", p=P))
+        nc.vector.memset(b_rows[H * D_TILES : P, :], 0.0)
 
+        one = keep.tile([P, 1], F32)
+        nc.vector.memset(one[:], 1.0)
+        warm = keep.tile([P, 1], F32)
+        nc.scalar.activation(out=warm[:], in_=one[:], func=ACT.Sqrt)
+
+        steps = [(b, pair) for b in range(B) for pair in range(PAIRS)]
         a_raw = {}
 
         def load_attn(b, pair):
@@ -68,11 +75,8 @@ def tile_multiheadattentionunit_pa_e_kernel(
                 in_=Wo_words[GROUPS * h : GROUPS * (h + 1)].rearrange("g p n t -> p g (n t)").bitcast(I32),
             )
 
-        load_attn(0, 0)
-
-        b_rows = keep.tile([P, P], BF16)
-        nc.vector.memset(b_rows[:], 0.0)
-        nc.scalar.dma_start(out=b_rows[0 : H * D_TILES, :], in_=bo.rearrange("h (t p) -> (h t) p", p=P))
+        load_attn(*steps[0])
+        load_attn(*steps[1])
 
         w_planes = keep.tile([P, PLANE_SETS, D], U8, align_bytes=64)
         nc.vector.memset(w_planes[:].bitcast(I32), 0)
@@ -84,22 +88,20 @@ def tile_multiheadattentionunit_pa_e_kernel(
                 )
 
         for pair in range(PAIRS):
-            if pair > 0:
-                load_attn(0, pair)
             for i in range(PAIR):
                 load_weight(PAIR * pair + i)
+            load_attn(*steps[pair + 2])
 
         q_sb = {}
         gamma_b = keep.tile([P, D], BF16)
         beta_b = keep.tile([P, D], BF16)
         for b in range(B):
             q_sb[b] = keep.tile([P, TOKEN_TILES, D], BF16, name="q_sb%d" % b)
-        load_attn(1, 0)
         nc.sync.dma_start(out=q_sb[0][:], in_=query_inputs[0].rearrange("(p r) d -> p r d", r=TOKEN_TILES))
         nc.sync.dma_start(out=gamma_b[:], in_=gamma.partition_broadcast(P))
         nc.sync.dma_start(out=beta_b[:], in_=beta.partition_broadcast(P))
-        for pair in range(1, PAIRS):
-            load_attn(1, pair)
+        for step in steps[PAIRS + 2 :]:
+            load_attn(*step)
         nc.sync.dma_start(out=q_sb[1][:], in_=query_inputs[1].rearrange("(p r) d -> p r d", r=TOKEN_TILES))
 
         b_rows32 = keep.tile([P, P], F32)
@@ -121,16 +123,15 @@ def tile_multiheadattentionunit_pa_e_kernel(
             out=bias_sum[:], in_=bias[:].rearrange("p h t -> p t h"), axis=mybir.AxisListType.X, op=ALU.add
         )
 
+        grouped = {}
         a_codes = {}
         a_scales = {}
         head_sum = {}
         for b in range(B):
             head_sum[b] = keep.tile([P, D_TILES, S], F32, name="head_sum%d" % b)
 
-        def quantise_pair(b, pair):
-            grouped = stage.tile([P, PAIR, GROUPS, S, 4], BF16, align_bytes=64)
-            a_codes[b, pair] = stage.tile([P, PAIR, GROUPS, S], U32, name="a_codes", align_bytes=64)
-            a_scales[b, pair] = stage.tile([P, PAIR, GROUPS, S], U8, name="a_scales", align_bytes=64)
+        def transpose_pair(b, pair):
+            grouped[b, pair] = stage.tile([P, PAIR, GROUPS, S, 4], BF16, name="grouped", align_bytes=64)
             for i in range(PAIR):
                 for g in range(GROUPS):
                     pairs_t = psum_t.tile([P, 2, S], F32, tag="t")
@@ -143,53 +144,66 @@ def tile_multiheadattentionunit_pa_e_kernel(
                                 ident[:],
                             )
                     nc.scalar.copy(
-                        out=grouped[:, i, g].rearrange("p n t -> p (n t)").bitcast(F32).rearrange("p (n u) -> p n u", u=2),
+                        out=grouped[b, pair][:, i, g]
+                        .rearrange("p n t -> p (n t)")
+                        .bitcast(F32)
+                        .rearrange("p (n u) -> p n u", u=2),
                         in_=pairs_t[:].rearrange("p u n -> p n u"),
                     )
+
+        def quantise_pair(b, pair):
+            a_codes[b, pair] = stage.tile([P, PAIR, GROUPS, S], U32, name="a_codes", align_bytes=64)
+            a_scales[b, pair] = stage.tile([P, PAIR, GROUPS, S], U8, name="a_scales", align_bytes=64)
             for i in range(PAIR):
                 nc.vector.quantize_mx(
                     out=a_codes[b, pair][:, i].rearrange("p g n -> p (g n)").bitcast(FP8X4),
                     scales=a_scales[b, pair][:, i].rearrange("p g n -> p (g n)"),
-                    in_=grouped[:, i].rearrange("p g n t -> p (g n t)"),
+                    in_=grouped[b, pair][:, i].rearrange("p g n t -> p (g n t)"),
                 )
 
-        def leave_psum(b, h, t, product):
-            total = head_sum[b][:, t, :]
-            if t % 3 == 1:
-                if h == 0:
-                    nc.scalar.activation(out=total, in_=product, func=ACT.Relu, bias=bias[:, h, t : t + 1])
-                else:
-                    term = terms.tile([P, S], F32)
-                    nc.scalar.activation(out=term[:], in_=product, func=ACT.Relu, bias=bias[:, h, t : t + 1])
-                    nc.gpsimd.tensor_tensor(out=total, in0=total, in1=term[:], op=ALU.add)
-            elif h == 0:
-                nc.vector.tensor_scalar(
-                    out=total,
-                    in0=product,
-                    scalar1=neg_bias[:, h, t : t + 1],
-                    scalar2=bias_sum[:, t : t + 1],
-                    op0=ALU.max,
-                    op1=ALU.add,
-                )
+        def leave_psum(b, h, first_t, products):
+            total = head_sum[b][:, first_t : first_t + PER_BANK, :]
+            if (first_t // PER_BANK) % 2 == 0:
+                term = total if h == 0 else terms.tile([P, PER_BANK, S], F32, name="term")[:]
+                for j in range(PER_BANK):
+                    t = first_t + j
+                    nc.scalar.activation(
+                        out=term[:, j, :], in_=products[:, j, :], func=ACT.Relu, bias=bias[:, h, t : t + 1]
+                    )
+                if h > 0:
+                    nc.gpsimd.tensor_tensor(out=total, in0=total, in1=term, op=ALU.add)
             else:
-                nc.vector.scalar_tensor_tensor(
-                    out=total,
-                    in0=product,
-                    scalar=neg_bias[:, h, t : t + 1],
-                    in1=total,
-                    op0=ALU.max,
-                    op1=ALU.add,
-                )
+                for j in range(PER_BANK):
+                    t = first_t + j
+                    if h == 0:
+                        nc.vector.tensor_scalar(
+                            out=total[:, j, :],
+                            in0=products[:, j, :],
+                            scalar1=neg_bias[:, h, t : t + 1],
+                            scalar2=bias_sum[:, t : t + 1],
+                            op0=ALU.max,
+                            op1=ALU.add,
+                        )
+                    else:
+                        nc.vector.scalar_tensor_tensor(
+                            out=total[:, j, :],
+                            in0=products[:, j, :],
+                            scalar=neg_bias[:, h, t : t + 1],
+                            in1=total[:, j, :],
+                            op0=ALU.max,
+                            op1=ALU.add,
+                        )
 
-        def multiply_pair(b, pair):
-            for i in range(PAIR):
-                h = PAIR * pair + i
-                for t in range(D_TILES):
-                    product = psum_mx.tile([P, S], F32)
+        def multiply_head(b, pair, i):
+            h = PAIR * pair + i
+            for first_t in range(0, D_TILES, PER_BANK):
+                products = psum_mx.tile([P, PER_BANK, S], F32)
+                for j in range(PER_BANK):
+                    t = first_t + j
                     for g in range(GROUPS):
                         plane_set, plane = divmod(GROUPS * h + g, PLANES)
                         nc.tensor.matmul_mx(
-                            out=product[:],
+                            out=products[:, j, :],
                             lhsT=w_words[h][:, g, P * t : P * (t + 1)].bitcast(FP8X4),
                             lhsT_scale=w_planes[4 * plane : P, plane_set, P * t : P * (t + 1)],
                             rhs=a_codes[b, pair][:, i, g, :].bitcast(FP8X4),
@@ -197,10 +211,17 @@ def tile_multiheadattentionunit_pa_e_kernel(
                             start=(g == 0),
                             stop=(g == GROUPS - 1),
                         )
-                    leave_psum(b, h, t, product[:])
+                leave_psum(b, h, first_t, products[:])
 
-        def layer_norm(b, r):
-            x = stage.tile([P, D], F32)
+        x = {}
+        y = {}
+        neg_mean = {}
+        std = {}
+
+        def norm_begin(b, r):
+            x[b, r] = stage.tile([P, D], F32, name="x")
+            y[b, r] = stage.tile([P, D], F32, name="y")
+            neg_mean[b, r] = small.tile([P, 1], F32, name="neg_mean")
             half_sums = small.tile([P, D // BANK], F32)
             for c in range(D // BANK):
                 x_t = psum_t.tile([P, BANK], F32, tag="t")
@@ -211,7 +232,7 @@ def tile_multiheadattentionunit_pa_e_kernel(
                         ident[:],
                     )
                 nc.vector.scalar_tensor_tensor(
-                    out=x[:, BANK * c : BANK * (c + 1)],
+                    out=x[b, r][:, BANK * c : BANK * (c + 1)],
                     in0=x_t[:],
                     scalar=1.0,
                     in1=q_sb[b][:, r, BANK * c : BANK * (c + 1)],
@@ -219,38 +240,53 @@ def tile_multiheadattentionunit_pa_e_kernel(
                     op1=ALU.add,
                     accum_out=half_sums[:, c : c + 1],
                 )
-            neg_mean = small.tile([P, 1], F32)
             nc.vector.tensor_scalar(
-                out=neg_mean[:],
+                out=neg_mean[b, r][:],
                 in0=half_sums[:, 0:1],
                 scalar1=half_sums[:, 1:2],
                 scalar2=-1.0 / D,
                 op0=ALU.add,
                 op1=ALU.mult,
             )
+            nc.vector.scalar_tensor_tensor(
+                out=y[b, r][:], in0=x[b, r][:], scalar=neg_mean[b, r][:], in1=gamma_b[:], op0=ALU.add, op1=ALU.mult
+            )
+
+        def norm_spread(b, r):
             squares = stage.tile([P, D], BF16)
             sum_sq = small.tile([P, 1], F32)
-            nc.scalar.activation(out=squares[:], in_=x[:], func=ACT.Square, bias=neg_mean[:], accum_out=sum_sq[:])
-            y = stage.tile([P, D], F32)
-            nc.vector.scalar_tensor_tensor(
-                out=y[:], in0=x[:], scalar=neg_mean[:], in1=gamma_b[:], op0=ALU.add, op1=ALU.mult
+            std[b, r] = small.tile([P, 1], F32, name="std")
+            nc.scalar.activation(
+                out=squares[:], in_=x[b, r][:], func=ACT.Square, bias=neg_mean[b, r][:], accum_out=sum_sq[:]
             )
-            std = small.tile([P, 1], F32)
-            nc.scalar.activation(out=std[:], in_=sum_sq[:], func=ACT.Sqrt, bias=eps[:], scale=1.0 / D)
-            rstd = small.tile([P, 1], F32)
-            nc.vector.reciprocal(out=rstd[:], in_=std[:])
-            nc.vector.scalar_tensor_tensor(
-                out=y[:], in0=y[:], scalar=rstd[:], in1=beta_b[:], op0=ALU.mult, op1=ALU.add
-            )
-            nc.sync.dma_start(out=out[b].rearrange("(p r) d -> p r d", r=TOKEN_TILES)[:, r, :], in_=y[:])
+            nc.scalar.activation(out=std[b, r][:], in_=sum_sq[:], func=ACT.Sqrt, bias=LN_EPS, scale=1.0 / D)
 
-        steps = [(b, pair) for b in range(B) for pair in range(PAIRS)]
+        def norm_finish(b, r):
+            rstd = small.tile([P, 1], F32)
+            nc.vector.reciprocal(out=rstd[:], in_=std[b, r][:])
+            nc.vector.scalar_tensor_tensor(
+                out=y[b, r][:], in0=y[b, r][:], scalar=rstd[:], in1=beta_b[:], op0=ALU.mult, op1=ALU.add
+            )
+            nc.sync.dma_start(out=out[b].rearrange("(p r) d -> p r d", r=TOKEN_TILES)[:, r, :], in_=y[b, r][:])
+
+        transpose_pair(*steps[0])
         quantise_pair(*steps[0])
         for n, (b, pair) in enumerate(steps):
+            norm_now = b > 0 and 1 <= pair <= TOKEN_TILES
+            if n + 1 < len(steps):
+                transpose_pair(*steps[n + 1])
+            multiply_head(b, pair, 0)
+            if norm_now:
+                norm_spread(b - 1, pair - 1)
             if n + 1 < len(steps):
                 quantise_pair(*steps[n + 1])
-            multiply_pair(b, pair)
+            if norm_now:
+                norm_finish(b - 1, pair - 1)
+            multiply_head(b, pair, 1)
             if b > 0 and pair < TOKEN_TILES:
-                layer_norm(b - 1, pair)
+                norm_begin(b - 1, pair)
         for r in range(TOKEN_TILES):
-            layer_norm(B - 1, r)
+            norm_begin(B - 1, r)
+        for r in range(TOKEN_TILES):
+            norm_spread(B - 1, r)
+            norm_finish(B - 1, r)

@@ -28,6 +28,7 @@ BANK = 512
 PER_BANK = BANK // S
 PLANES = 4
 PLANE_SETS = H * GROUPS // PLANES
+assert PLANES == PAIR * GROUPS and PLANE_SETS == PAIRS
 
 
 def tile_multiheadattentionunit_pa_e_kernel(
@@ -75,22 +76,27 @@ def tile_multiheadattentionunit_pa_e_kernel(
                 in_=Wo_words[GROUPS * h : GROUPS * (h + 1)].rearrange("g p n t -> p g (n t)").bitcast(I32),
             )
 
-        load_attn(*steps[0])
-        load_attn(*steps[1])
-
         w_planes = keep.tile([P, PLANE_SETS, D], U8, align_bytes=64)
         nc.vector.memset(w_planes[:].bitcast(I32), 0)
-        for j in range(PLANE_SETS):
+
+        def load_planes(pair):
             for quadrant in range(4):
                 nc.sync.dma_start(
-                    out=w_planes[32 * quadrant : 32 * quadrant + 4 * PLANES, j, :].bitcast(I32),
-                    in_=Wo_scales[PLANES * j : PLANES * (j + 1), 4 * quadrant : 4 * quadrant + 4, :].bitcast(I32),
+                    out=w_planes[32 * quadrant : 32 * quadrant + 4 * PLANES, pair, :].bitcast(I32),
+                    in_=Wo_scales[PLANES * pair : PLANES * (pair + 1), 4 * quadrant : 4 * quadrant + 4, :].bitcast(I32),
                 )
 
+        load_attn(*steps[0])
+        load_planes(0)
+        load_attn(*steps[1])
         for pair in range(PAIRS):
             for i in range(PAIR):
                 load_weight(PAIR * pair + i)
             load_attn(*steps[pair + 2])
+            if pair + 1 < PAIRS:
+                load_planes(pair + 1)
+        for step in steps[PAIRS + 2 :]:
+            load_attn(*step)
 
         q_sb = {}
         gamma_b = keep.tile([P, D], BF16)
@@ -100,8 +106,6 @@ def tile_multiheadattentionunit_pa_e_kernel(
         nc.sync.dma_start(out=q_sb[0][:], in_=query_inputs[0].rearrange("(p r) d -> p r d", r=TOKEN_TILES))
         nc.sync.dma_start(out=gamma_b[:], in_=gamma.partition_broadcast(P))
         nc.sync.dma_start(out=beta_b[:], in_=beta.partition_broadcast(P))
-        for step in steps[PAIRS + 2 :]:
-            load_attn(*step)
         nc.sync.dma_start(out=q_sb[1][:], in_=query_inputs[1].rearrange("(p r) d -> p r d", r=TOKEN_TILES))
 
         b_rows32 = keep.tile([P, P], F32)
@@ -272,19 +276,20 @@ def tile_multiheadattentionunit_pa_e_kernel(
         transpose_pair(*steps[0])
         quantise_pair(*steps[0])
         for n, (b, pair) in enumerate(steps):
-            norm_now = b > 0 and 1 <= pair <= TOKEN_TILES
+            ending = pair - 2
+            starting = pair - 1
             if n + 1 < len(steps):
                 transpose_pair(*steps[n + 1])
             multiply_head(b, pair, 0)
-            if norm_now:
-                norm_spread(b - 1, pair - 1)
+            if b > 0 and 0 <= ending < TOKEN_TILES:
+                norm_spread(b - 1, ending)
             if n + 1 < len(steps):
                 quantise_pair(*steps[n + 1])
-            if norm_now:
-                norm_finish(b - 1, pair - 1)
+            if b > 0 and 0 <= ending < TOKEN_TILES:
+                norm_finish(b - 1, ending)
             multiply_head(b, pair, 1)
-            if b > 0 and pair < TOKEN_TILES:
-                norm_begin(b - 1, pair)
+            if b > 0 and 0 <= starting < TOKEN_TILES:
+                norm_begin(b - 1, starting)
         for r in range(TOKEN_TILES):
             norm_begin(B - 1, r)
         for r in range(TOKEN_TILES):

@@ -56,7 +56,7 @@ def tile_multiheadattentionunit_pa_e_kernel(
         warm = keep.tile([P, 1], F32)
         nc.scalar.activation(out=warm[:], in_=one[:], func=ACT.Sqrt)
 
-        steps = [(b, pair) for b in range(B) for pair in range(PAIRS)]
+        steps = [(0, 0), (1, 0)] + [(b, pair) for b in range(B) for pair in range(1, PAIRS)]
         a_raw = {}
 
         def load_attn(b, pair):
@@ -87,16 +87,13 @@ def tile_multiheadattentionunit_pa_e_kernel(
                 )
 
         load_attn(*steps[0])
-        load_planes(0)
-        load_attn(*steps[1])
-        for pair in range(PAIRS):
-            for i in range(PAIR):
-                load_weight(PAIR * pair + i)
-            load_attn(*steps[pair + 2])
-            if pair + 1 < PAIRS:
-                load_planes(pair + 1)
-        for step in steps[PAIRS + 2 :]:
-            load_attn(*step)
+        for n, (b, pair) in enumerate(steps):
+            if n + 1 < len(steps):
+                load_attn(*steps[n + 1])
+            if b == 0:
+                load_planes(pair)
+                for i in range(PAIR):
+                    load_weight(PAIR * pair + i)
 
         q_sb = {}
         gamma_b = keep.tile([P, D], BF16)

@@ -56,16 +56,13 @@ def tile_multiheadattentionunit_pa_e_kernel(
         warm = keep.tile([P, 1], F32)
         nc.scalar.activation(out=warm[:], in_=one[:], func=ACT.Sqrt)
 
-        steps = [(0, 0), (1, 0)] + [(b, pair) for b in range(B) for pair in range(1, PAIRS)]
+        steps = [[(b, h) for b in range(B)] for h in range(PAIR)]
+        steps += [[(b, PAIR * pair + i) for i in range(PAIR)] for b in range(B) for pair in range(1, PAIRS)]
         a_raw = {}
 
-        def load_attn(b, pair):
-            a_raw[b, pair] = keep.tile([P, PAIR, TOKEN_TILES, DV], BF16, name="a_raw%d_%d" % (b, pair))
-            for i in range(PAIR):
-                nc.sync.dma_start(
-                    out=a_raw[b, pair][:, i],
-                    in_=attn[b, PAIR * pair + i].rearrange("(p r) k -> p r k", r=TOKEN_TILES),
-                )
+        def load_attn(b, h):
+            a_raw[b, h] = keep.tile([P, TOKEN_TILES, DV], BF16, name="a_raw%d_%d" % (b, h))
+            nc.sync.dma_start(out=a_raw[b, h][:], in_=attn[b, h].rearrange("(p r) k -> p r k", r=TOKEN_TILES))
 
         w_words = {}
 
@@ -86,14 +83,23 @@ def tile_multiheadattentionunit_pa_e_kernel(
                     in_=Wo_scales[PLANES * pair : PLANES * (pair + 1), 4 * quadrant : 4 * quadrant + 4, :].bitcast(I32),
                 )
 
-        load_attn(*steps[0])
-        for n, (b, pair) in enumerate(steps):
+        for h in range(PAIR):
+            for unit in steps[h]:
+                load_attn(*unit)
+            if h == 0:
+                load_planes(0)
+            load_weight(h)
+        for unit in steps[PAIR]:
+            load_attn(*unit)
+        for n in range(PAIR, len(steps)):
             if n + 1 < len(steps):
-                load_attn(*steps[n + 1])
+                for unit in steps[n + 1]:
+                    load_attn(*unit)
+            b, h = steps[n][0]
             if b == 0:
-                load_planes(pair)
+                load_planes(h // PAIR)
                 for i in range(PAIR):
-                    load_weight(PAIR * pair + i)
+                    load_weight(h + i)
 
         q_sb = {}
         gamma_b = keep.tile([P, D], BF16)
@@ -131,35 +137,35 @@ def tile_multiheadattentionunit_pa_e_kernel(
         for b in range(B):
             head_sum[b] = keep.tile([P, D_TILES, S], F32, name="head_sum%d" % b)
 
-        def transpose_pair(b, pair):
-            grouped[b, pair] = stage.tile([P, PAIR, GROUPS, S, 4], BF16, name="grouped", align_bytes=64)
-            for i in range(PAIR):
+        def transpose_step(n):
+            grouped[n] = stage.tile([P, PAIR, GROUPS, S, 4], BF16, name="grouped", align_bytes=64)
+            for i, unit in enumerate(steps[n]):
                 for g in range(GROUPS):
                     pairs_t = psum_t.tile([P, 2, S], F32, tag="t")
                     for u in range(2):
                         for r in range(TOKEN_TILES):
-                            words = a_raw[b, pair][:, i, r, :].bitcast(F32)
+                            words = a_raw[unit][:, r, :].bitcast(F32)
                             nc.tensor.transpose(
                                 pairs_t[:, u, P * r : P * (r + 1)],
                                 words[:, WORDS * g + u : WORDS * (g + 1) : 2],
                                 ident[:],
                             )
                     nc.scalar.copy(
-                        out=grouped[b, pair][:, i, g]
+                        out=grouped[n][:, i, g]
                         .rearrange("p n t -> p (n t)")
                         .bitcast(F32)
                         .rearrange("p (n u) -> p n u", u=2),
                         in_=pairs_t[:].rearrange("p u n -> p n u"),
                     )
 
-        def quantise_pair(b, pair):
-            a_codes[b, pair] = stage.tile([P, PAIR, GROUPS, S], U32, name="a_codes", align_bytes=64)
-            a_scales[b, pair] = stage.tile([P, PAIR, GROUPS, S], U8, name="a_scales", align_bytes=64)
+        def quantise_step(n):
+            a_codes[n] = stage.tile([P, PAIR, GROUPS, S], U32, name="a_codes", align_bytes=64)
+            a_scales[n] = stage.tile([P, PAIR, GROUPS, S], U8, name="a_scales", align_bytes=64)
             for i in range(PAIR):
                 nc.vector.quantize_mx(
-                    out=a_codes[b, pair][:, i].rearrange("p g n -> p (g n)").bitcast(FP8X4),
-                    scales=a_scales[b, pair][:, i].rearrange("p g n -> p (g n)"),
-                    in_=grouped[b, pair][:, i].rearrange("p g n t -> p (g n t)"),
+                    out=a_codes[n][:, i].rearrange("p g n -> p (g n)").bitcast(FP8X4),
+                    scales=a_scales[n][:, i].rearrange("p g n -> p (g n)"),
+                    in_=grouped[n][:, i].rearrange("p g n t -> p (g n t)"),
                 )
 
         def leave_psum(b, h, first_t, products):
@@ -195,8 +201,8 @@ def tile_multiheadattentionunit_pa_e_kernel(
                             op1=ALU.add,
                         )
 
-        def multiply_head(b, pair, i):
-            h = PAIR * pair + i
+        def multiply_unit(n, i):
+            b, h = steps[n][i]
             for first_t in range(0, D_TILES, PER_BANK):
                 products = psum_mx.tile([P, PER_BANK, S], F32)
                 for j in range(PER_BANK):
@@ -207,8 +213,8 @@ def tile_multiheadattentionunit_pa_e_kernel(
                             out=products[:, j, :],
                             lhsT=w_words[h][:, g, P * t : P * (t + 1)].bitcast(FP8X4),
                             lhsT_scale=w_planes[4 * plane : P, plane_set, P * t : P * (t + 1)],
-                            rhs=a_codes[b, pair][:, i, g, :].bitcast(FP8X4),
-                            rhs_scale=a_scales[b, pair][:, i, g, :],
+                            rhs=a_codes[n][:, i, g, :].bitcast(FP8X4),
+                            rhs_scale=a_scales[n][:, i, g, :],
                             start=(g == 0),
                             stop=(g == GROUPS - 1),
                         )
@@ -270,21 +276,26 @@ def tile_multiheadattentionunit_pa_e_kernel(
             )
             nc.sync.dma_start(out=out[b].rearrange("(p r) d -> p r d", r=TOKEN_TILES)[:, r, :], in_=y[b, r][:])
 
-        transpose_pair(*steps[0])
-        quantise_pair(*steps[0])
-        for n, (b, pair) in enumerate(steps):
+        transpose_step(0)
+        quantise_step(0)
+        for n in range(len(steps)):
+            b, h = steps[n][0]
+            pair = h // PAIR
             ending = pair - 2
             starting = pair - 1
+            if n == 0:
+                multiply_unit(n, 0)
             if n + 1 < len(steps):
-                transpose_pair(*steps[n + 1])
-            multiply_head(b, pair, 0)
+                transpose_step(n + 1)
+            if n > 0:
+                multiply_unit(n, 0)
             if b > 0 and 0 <= ending < TOKEN_TILES:
                 norm_spread(b - 1, ending)
             if n + 1 < len(steps):
-                quantise_pair(*steps[n + 1])
+                quantise_step(n + 1)
             if b > 0 and 0 <= ending < TOKEN_TILES:
                 norm_finish(b - 1, ending)
-            multiply_head(b, pair, 1)
+            multiply_unit(n, 1)
             if b > 0 and 0 <= starting < TOKEN_TILES:
                 norm_begin(b - 1, starting)
         for r in range(TOKEN_TILES):

@@ -137,9 +137,11 @@ def tile_multiheadattentionunit_pa_e_kernel(
         for b in range(B):
             head_sum[b] = keep.tile([P, D_TILES, S], F32, name="head_sum%d" % b)
 
-        def transpose_step(n):
-            grouped[n] = stage.tile([P, PAIR, GROUPS, S, 4], BF16, name="grouped", align_bytes=64)
-            for i, unit in enumerate(steps[n]):
+        def transpose_unit(n, i):
+            if i == 0:
+                grouped[n] = stage.tile([P, PAIR, GROUPS, S, 4], BF16, name="grouped", align_bytes=64)
+            unit = steps[n][i]
+            if True:
                 for g in range(GROUPS):
                     pairs_t = psum_t.tile([P, 2, S], F32, tag="t")
                     for u in range(2):
@@ -158,10 +160,11 @@ def tile_multiheadattentionunit_pa_e_kernel(
                         in_=pairs_t[:].rearrange("p u n -> p n u"),
                     )
 
-        def quantise_step(n):
-            a_codes[n] = stage.tile([P, PAIR, GROUPS, S], U32, name="a_codes", align_bytes=64)
-            a_scales[n] = stage.tile([P, PAIR, GROUPS, S], U8, name="a_scales", align_bytes=64)
-            for i in range(PAIR):
+        def quantise_unit(n, i):
+            if i == 0:
+                a_codes[n] = stage.tile([P, PAIR, GROUPS, S], U32, name="a_codes", align_bytes=64)
+                a_scales[n] = stage.tile([P, PAIR, GROUPS, S], U8, name="a_scales", align_bytes=64)
+            if True:
                 nc.vector.quantize_mx(
                     out=a_codes[n][:, i].rearrange("p g n -> p (g n)").bitcast(FP8X4),
                     scales=a_scales[n][:, i].rearrange("p g n -> p (g n)"),
@@ -276,28 +279,29 @@ def tile_multiheadattentionunit_pa_e_kernel(
             )
             nc.sync.dma_start(out=out[b].rearrange("(p r) d -> p r d", r=TOKEN_TILES)[:, r, :], in_=y[b, r][:])
 
-        transpose_step(0)
-        quantise_step(0)
+        for i in range(PAIR):
+            transpose_unit(0, i)
+        for i in range(PAIR):
+            quantise_unit(0, i)
         for n in range(len(steps)):
             b, h = steps[n][0]
             pair = h // PAIR
             ending = pair - 2
             starting = pair - 1
-            if n == 0:
-                multiply_unit(n, 0)
-            if n + 1 < len(steps):
-                transpose_step(n + 1)
-            if n > 0:
-                multiply_unit(n, 0)
+            multiply_unit(n, 0)
             if b > 0 and 0 <= ending < TOKEN_TILES:
                 norm_spread(b - 1, ending)
             if n + 1 < len(steps):
-                quantise_step(n + 1)
+                transpose_unit(n + 1, 0)
+                quantise_unit(n + 1, 0)
             if b > 0 and 0 <= ending < TOKEN_TILES:
                 norm_finish(b - 1, ending)
             multiply_unit(n, 1)
             if b > 0 and 0 <= starting < TOKEN_TILES:
                 norm_begin(b - 1, starting)
+            if n + 1 < len(steps):
+                transpose_unit(n + 1, 1)
+                quantise_unit(n + 1, 1)
         for r in range(TOKEN_TILES):
             norm_begin(B - 1, r)
         for r in range(TOKEN_TILES):

@@ -204,7 +204,7 @@ def tile_multiheadattentionunit_pa_e_kernel(
                             op1=ALU.add,
                         )
 
-        def multiply_unit(n, i):
+        def multiply_unit(n, i, behind_bank):
             b, h = steps[n][i]
             for first_t in range(0, D_TILES, PER_BANK):
                 products = psum_mx.tile([P, PER_BANK, S], F32)
@@ -222,28 +222,34 @@ def tile_multiheadattentionunit_pa_e_kernel(
                             stop=(g == GROUPS - 1),
                         )
                 leave_psum(b, h, first_t, products[:])
+                for piece in behind_bank.get(first_t // PER_BANK, []):
+                    piece[0](*piece[1:])
 
+        x_t = {}
         x = {}
         y = {}
         neg_mean = {}
         std = {}
 
-        def norm_begin(b, r):
-            x[b, r] = stage.tile([P, D], F32, name="x")
-            y[b, r] = stage.tile([P, D], F32, name="y")
-            neg_mean[b, r] = small.tile([P, 1], F32, name="neg_mean")
-            half_sums = small.tile([P, D // BANK], F32)
+        def norm_turn(b, r):
             for c in range(D // BANK):
-                x_t = psum_t.tile([P, BANK], F32, tag="t")
+                bank = psum_t.tile([P, BANK], F32, tag="t")
+                x_t[b, r, c] = bank
                 for j in range(BANK // P):
                     nc.tensor.transpose(
-                        x_t[:, P * j : P * (j + 1)],
+                        bank[:, P * j : P * (j + 1)],
                         head_sum[b][:, (BANK // P) * c + j, P * r : P * (r + 1)],
                         ident[:],
                     )
+
+        def norm_sum(b, r):
+            x[b, r] = stage.tile([P, D], F32, name="x")
+            neg_mean[b, r] = small.tile([P, 1], F32, name="neg_mean")
+            half_sums = small.tile([P, D // BANK], F32)
+            for c in range(D // BANK):
                 nc.vector.scalar_tensor_tensor(
                     out=x[b, r][:, BANK * c : BANK * (c + 1)],
-                    in0=x_t[:],
+                    in0=x_t[b, r, c][:],
                     scalar=1.0,
                     in1=q_sb[b][:, r, BANK * c : BANK * (c + 1)],
                     op0=ALU.mult,
@@ -258,6 +264,9 @@ def tile_multiheadattentionunit_pa_e_kernel(
                 op0=ALU.add,
                 op1=ALU.mult,
             )
+
+        def norm_scale(b, r):
+            y[b, r] = stage.tile([P, D], F32, name="y")
             nc.vector.scalar_tensor_tensor(
                 out=y[b, r][:], in0=x[b, r][:], scalar=neg_mean[b, r][:], in1=gamma_b[:], op0=ALU.add, op1=ALU.mult
             )
@@ -283,27 +292,21 @@ def tile_multiheadattentionunit_pa_e_kernel(
             transpose_unit(0, i)
         for i in range(PAIR):
             quantise_unit(0, i)
-        for n in range(len(steps)):
-            b, h = steps[n][0]
-            pair = h // PAIR
-            ending = pair - 2
-            starting = pair - 1
-            multiply_unit(n, 0)
-            if b > 0 and 0 <= ending < TOKEN_TILES:
-                norm_spread(b - 1, ending)
-            if n + 1 < len(steps):
-                transpose_unit(n + 1, 0)
-                quantise_unit(n + 1, 0)
-            if b > 0 and 0 <= ending < TOKEN_TILES:
-                norm_finish(b - 1, ending)
-            multiply_unit(n, 1)
-            if b > 0 and 0 <= starting < TOKEN_TILES:
-                norm_begin(b - 1, starting)
-            if n + 1 < len(steps):
-                transpose_unit(n + 1, 1)
-                quantise_unit(n + 1, 1)
+        after_0 = 1 + max([n for n in range(len(steps)) if steps[n][0][0] == 0])
+        pieces = {}
         for r in range(TOKEN_TILES):
-            norm_begin(B - 1, r)
+            pieces[after_0 + r, 1] = {1: [(norm_turn, 0, r)], 3: [(norm_sum, 0, r)]}
+            pieces[after_0 + r + 1, 0] = {1: [(norm_scale, 0, r), (norm_spread, 0, r)], 3: [(norm_finish, 0, r)]}
+        for n in range(len(steps)):
+            for i in range(PAIR):
+                multiply_unit(n, i, pieces.get((n, i), {}))
+                if n + 1 < len(steps):
+                    transpose_unit(n + 1, i)
+                    quantise_unit(n + 1, i)
+        for r in range(TOKEN_TILES):
+            norm_turn(B - 1, r)
+            norm_sum(B - 1, r)
+            norm_scale(B - 1, r)
         for r in range(TOKEN_TILES):
             norm_spread(B - 1, r)
             norm_finish(B - 1, r)

@@ -46,6 +46,8 @@ def tile_multiheadattentionunit_pa_e_kernel(
 
         ident = keep.tile([P, P], F32)
         make_identity(nc, ident[:])
+        ident_bf = keep.tile([P, P], BF16)
+        make_identity(nc, ident_bf[:])
 
         b_rows = keep.tile([P, P], BF16)
         nc.sync.dma_start(out=b_rows[0 : H * D_TILES, :], in_=bo.rearrange("h (t p) -> (h t) p", p=P))
@@ -58,6 +60,9 @@ def tile_multiheadattentionunit_pa_e_kernel(
 
         steps = [[(b, h) for b in range(B)] for h in range(PAIR)]
         steps += [[(b, PAIR * pair + i) for i in range(PAIR)] for b in range(B) for pair in range(1, PAIRS)]
+        def by_scalar(b, h, bank):
+            return bank % 2 == 0 and not (bank > 0 and b == B - 1 and h in (0, H - 1))
+
         a_raw = {}
 
         def load_attn(b, h):
@@ -117,7 +122,7 @@ def tile_multiheadattentionunit_pa_e_kernel(
         nc.tensor.transpose(b_cols[:], b_rows32[:], ident[:])
         bias = keep.tile([P, H, D_TILES], F32)
         neg_bias = keep.tile([P, H, D_TILES], F32)
-        bias_sum = keep.tile([P, D_TILES], F32)
+        bias_sum = {}
         nc.vector.tensor_copy(out=bias[:].rearrange("p h t -> p (h t)"), in_=b_cols[:, 0 : H * D_TILES])
         nc.vector.tensor_scalar(
             out=neg_bias[:].rearrange("p h t -> p (h t)"),
@@ -126,9 +131,19 @@ def tile_multiheadattentionunit_pa_e_kernel(
             scalar2=None,
             op0=ALU.mult,
         )
-        nc.vector.tensor_reduce(
-            out=bias_sum[:], in_=bias[:].rearrange("p h t -> p t h"), axis=mybir.AxisListType.X, op=ALU.add
-        )
+        for b in range(B):
+            bias_sum[b] = keep.tile([P, D_TILES], F32, name="bias_sum%d" % b)
+            nc.vector.tensor_reduce(
+                out=bias_sum[b][:], in_=bias[:].rearrange("p h t -> p t h"), axis=mybir.AxisListType.X, op=ALU.add
+            )
+            for bank in range(D_TILES // PER_BANK):
+                heads = [h for h in range(H) if not by_scalar(b, h, bank)]
+                if 0 < len(heads) < H:
+                    assert len(heads) == 2
+                    d_tiles = slice(PER_BANK * bank, PER_BANK * (bank + 1))
+                    nc.vector.tensor_tensor(
+                        out=bias_sum[b][:, d_tiles], in0=bias[:, heads[0], d_tiles], in1=bias[:, heads[1], d_tiles], op=ALU.add
+                    )
 
         grouped = {}
         a_codes = {}
@@ -173,7 +188,7 @@ def tile_multiheadattentionunit_pa_e_kernel(
 
         def leave_psum(b, h, first_t, products):
             total = head_sum[b][:, first_t : first_t + PER_BANK, :]
-            if (first_t // PER_BANK) % 2 == 0:
+            if by_scalar(b, h, first_t // PER_BANK):
                 term = total if h == 0 else terms.tile([P, PER_BANK, S], F32, name="term")[:]
                 for j in range(PER_BANK):
                     t = first_t + j
@@ -190,7 +205,7 @@ def tile_multiheadattentionunit_pa_e_kernel(
                             out=total[:, j, :],
                             in0=products[:, j, :],
                             scalar1=neg_bias[:, h, t : t + 1],
-                            scalar2=bias_sum[:, t : t + 1],
+                            scalar2=bias_sum[b][:, t : t + 1],
                             op0=ALU.max,
                             op1=ALU.add,
                         )
@@ -242,6 +257,51 @@ def tile_multiheadattentionunit_pa_e_kernel(
                         ident[:],
                     )
 
+        def norm_seed(b, r):
+            for c in range(D // BANK):
+                bank = psum_t.tile([P, BANK], F32, tag="t")
+                x_t[b, r, c] = bank
+                nc.tensor.matmul(
+                    bank[:], lhsT=ident_bf[:], rhs=q_sb[b][:, r, BANK * c : BANK * (c + 1)], start=True, stop=False
+                )
+
+        def norm_turn_onto(b, r):
+            for c in range(D // BANK):
+                for j in range(BANK // P):
+                    nc.tensor.matmul(
+                        x_t[b, r, c][:, P * j : P * (j + 1)],
+                        lhsT=head_sum[b][:, (BANK // P) * c + j, P * r : P * (r + 1)],
+                        rhs=ident[:],
+                        is_transpose=True,
+                        start=False,
+                        stop=(j == BANK // P - 1),
+                    )
+
+        def norm_sum_seeded(b, r):
+            x[b, r] = stage.tile([P, D], F32, name="x")
+            neg_mean[b, r] = small.tile([P, 1], F32, name="neg_mean")
+            half_sums = small.tile([P, D // BANK], F32)
+            nc.scalar.activation(
+                out=x[b, r][:, 0:BANK], in_=x_t[b, r, 0][:], func=ACT.Identity, accum_out=half_sums[:, 0:1]
+            )
+            nc.vector.tensor_scalar(
+                out=x[b, r][:, BANK : 2 * BANK],
+                in0=x_t[b, r, 1][:],
+                scalar1=1.0,
+                scalar2=None,
+                op0=ALU.mult,
+                op1=ALU.add,
+                accum_out=half_sums[:, 1:2],
+            )
+            nc.vector.tensor_scalar(
+                out=neg_mean[b, r][:],
+                in0=half_sums[:, 0:1],
+                scalar1=half_sums[:, 1:2],
+                scalar2=-1.0 / D,
+                op0=ALU.add,
+                op1=ALU.mult,
+            )
+
         def norm_sum(b, r):
             x[b, r] = stage.tile([P, D], F32, name="x")
             neg_mean[b, r] = small.tile([P, 1], F32, name="neg_mean")
@@ -280,13 +340,17 @@ def tile_multiheadattentionunit_pa_e_kernel(
             )
             nc.scalar.activation(out=std[b, r][:], in_=sum_sq[:], func=ACT.Sqrt, bias=LN_EPS, scale=1.0 / D)
 
-        def norm_finish(b, r):
+        def norm_finish(b, r, pieces=1):
             rstd = small.tile([P, 1], F32)
             nc.vector.reciprocal(out=rstd[:], in_=std[b, r][:])
-            nc.vector.scalar_tensor_tensor(
-                out=y[b, r][:], in0=y[b, r][:], scalar=rstd[:], in1=beta_b[:], op0=ALU.mult, op1=ALU.add
-            )
-            nc.sync.dma_start(out=out[b].rearrange("(p r) d -> p r d", r=TOKEN_TILES)[:, r, :], in_=y[b, r][:])
+            for piece in range(pieces):
+                cols = slice(D // pieces * piece, D // pieces * (piece + 1))
+                nc.vector.scalar_tensor_tensor(
+                    out=y[b, r][:, cols], in0=y[b, r][:, cols], scalar=rstd[:], in1=beta_b[:, cols], op0=ALU.mult, op1=ALU.add
+                )
+                nc.sync.dma_start(
+                    out=out[b].rearrange("(p r) d -> p r d", r=TOKEN_TILES)[:, r, cols], in_=y[b, r][:, cols]
+                )
 
         for i in range(PAIR):
             transpose_unit(0, i)
@@ -304,9 +368,11 @@ def tile_multiheadattentionunit_pa_e_kernel(
                     transpose_unit(n + 1, i)
                     quantise_unit(n + 1, i)
         for r in range(TOKEN_TILES):
-            norm_turn(B - 1, r)
-            norm_sum(B - 1, r)
+            norm_seed(B - 1, r)
+        for r in range(TOKEN_TILES):
+            norm_turn_onto(B - 1, r)
+            norm_sum_seeded(B - 1, r)
             norm_scale(B - 1, r)
         for r in range(TOKEN_TILES):
             norm_spread(B - 1, r)
-            norm_finish(B - 1, r)
+            norm_finish(B - 1, r, 2)

@@ -72,11 +72,18 @@ def tile_multiheadattentionunit_pa_e_kernel(
         w_words = {}
 
         def load_weight(h):
-            w_words[h] = keep.tile([P, GROUPS, D], U32, name="w_words%d" % h, align_bytes=64)
-            nc.sync.dma_start(
-                out=w_words[h][:].bitcast(I32),
-                in_=Wo_words[GROUPS * h : GROUPS * (h + 1)].rearrange("g p n t -> p g (n t)").bitcast(I32),
-            )
+            loads = D_TILES // PER_BANK if h == 0 else 1
+            width = D // loads
+            w_words[h] = []
+            for k in range(loads):
+                piece = keep.tile([P, GROUPS, width], U32, name="w_words%d_%d" % (h, k), align_bytes=64)
+                w_words[h].append(piece)
+                nc.sync.dma_start(
+                    out=piece[:].bitcast(I32),
+                    in_=Wo_words[GROUPS * h : GROUPS * (h + 1)]
+                    .rearrange("g p n t -> p g (n t)")[:, :, 4 * width * k : 4 * width * (k + 1)]
+                    .bitcast(I32),
+                )
 
         w_planes = keep.tile([P, PLANE_SETS, D], U8, align_bytes=64)
         nc.vector.memset(w_planes[:].bitcast(I32), 0)
@@ -94,9 +101,18 @@ def tile_multiheadattentionunit_pa_e_kernel(
             if h == 0:
                 load_planes(0)
             load_weight(h)
+        q_sb = {}
+        gamma_b = keep.tile([P, D], BF16)
+        beta_b = keep.tile([P, D], BF16)
+        for b in range(B):
+            q_sb[b] = keep.tile([P, TOKEN_TILES, D], BF16, name="q_sb%d" % b)
         for unit in steps[PAIR]:
             load_attn(*unit)
         for n in range(PAIR, len(steps)):
+            if n + 1 == len(steps) - 1:
+                nc.sync.dma_start(out=q_sb[0][:], in_=query_inputs[0].rearrange("(p r) d -> p r d", r=TOKEN_TILES))
+                nc.sync.dma_start(out=gamma_b[:], in_=gamma.partition_broadcast(P))
+                nc.sync.dma_start(out=beta_b[:], in_=beta.partition_broadcast(P))
             if n + 1 < len(steps):
                 for unit in steps[n + 1]:
                     load_attn(*unit)
@@ -105,15 +121,6 @@ def tile_multiheadattentionunit_pa_e_kernel(
                 load_planes(h // PAIR)
                 for i in range(PAIR):
                     load_weight(h + i)
-
-        q_sb = {}
-        gamma_b = keep.tile([P, D], BF16)
-        beta_b = keep.tile([P, D], BF16)
-        for b in range(B):
-            q_sb[b] = keep.tile([P, TOKEN_TILES, D], BF16, name="q_sb%d" % b)
-        nc.sync.dma_start(out=q_sb[0][:], in_=query_inputs[0].rearrange("(p r) d -> p r d", r=TOKEN_TILES))
-        nc.sync.dma_start(out=gamma_b[:], in_=gamma.partition_broadcast(P))
-        nc.sync.dma_start(out=beta_b[:], in_=beta.partition_broadcast(P))
         nc.sync.dma_start(out=q_sb[1][:], in_=query_inputs[1].rearrange("(p r) d -> p r d", r=TOKEN_TILES))
 
         b_rows32 = keep.tile([P, P], F32)
@@ -227,9 +234,10 @@ def tile_multiheadattentionunit_pa_e_kernel(
                     t = first_t + j
                     for g in range(GROUPS):
                         plane_set, plane = divmod(GROUPS * h + g, PLANES)
+                        k, t_in_piece = divmod(t, D_TILES // len(w_words[h]))
                         nc.tensor.matmul_mx(
                             out=products[:, j, :],
-                            lhsT=w_words[h][:, g, P * t : P * (t + 1)].bitcast(FP8X4),
+                            lhsT=w_words[h][k][:, g, P * t_in_piece : P * (t_in_piece + 1)].bitcast(FP8X4),
                             lhsT_scale=w_planes[4 * plane : P, plane_set, P * t : P * (t + 1)],
                             rhs=a_codes[n][:, i, g, :].bitcast(FP8X4),
                             rhs_scale=a_scales[n][:, i, g, :],
@@ -359,8 +367,9 @@ def tile_multiheadattentionunit_pa_e_kernel(
         after_0 = 1 + max([n for n in range(len(steps)) if steps[n][0][0] == 0])
         pieces = {}
         for r in range(TOKEN_TILES):
-            pieces[after_0 + r, 1] = {1: [(norm_turn, 0, r)], 3: [(norm_sum, 0, r)]}
-            pieces[after_0 + r + 1, 0] = {1: [(norm_scale, 0, r), (norm_spread, 0, r)], 3: [(norm_finish, 0, r)]}
+            pieces[after_0 + r, 0] = {1: [(norm_turn, 0, r)], 3: [(norm_sum, 0, r)]}
+            pieces[after_0 + r, 1] = {1: [(norm_scale, 0, r), (norm_spread, 0, r)], 3: [(norm_finish, 0, r)]}
+        pieces[after_0 + 1, 0][1] = pieces[after_0, 1].pop(3) + pieces[after_0 + 1, 0][1]
         for n in range(len(steps)):
             for i in range(PAIR):
                 multiply_unit(n, i, pieces.get((n, i), {}))
@@ -375,4 +384,4 @@ def tile_multiheadattentionunit_pa_e_kernel(
             norm_scale(B - 1, r)
         for r in range(TOKEN_TILES):
             norm_spread(B - 1, r)
-            norm_finish(B - 1, r, 2)
+            norm_finish(B - 1, r, 2 * (r + 1))

@@ -106,19 +106,17 @@ def tile_multiheadattentionunit_pa_e_kernel(
         beta_b = keep.tile([P, D], BF16)
         for b in range(B):
             q_sb[b] = keep.tile([P, TOKEN_TILES, D], BF16, name="q_sb%d" % b)
-        for unit in steps[PAIR]:
-            load_attn(*unit)
+        for pair in range(1, PAIRS):
+            load_planes(pair)
         for n in range(PAIR, len(steps)):
-            if n + 1 == len(steps) - 1:
+            if n == len(steps) - 1:
                 nc.sync.dma_start(out=q_sb[0][:], in_=query_inputs[0].rearrange("(p r) d -> p r d", r=TOKEN_TILES))
                 nc.sync.dma_start(out=gamma_b[:], in_=gamma.partition_broadcast(P))
                 nc.sync.dma_start(out=beta_b[:], in_=beta.partition_broadcast(P))
-            if n + 1 < len(steps):
-                for unit in steps[n + 1]:
-                    load_attn(*unit)
+            for unit in steps[n]:
+                load_attn(*unit)
             b, h = steps[n][0]
             if b == 0:
-                load_planes(h // PAIR)
                 for i in range(PAIR):
                     load_weight(h + i)
         nc.sync.dma_start(out=q_sb[1][:], in_=query_inputs[1].rearrange("(p r) d -> p r d", r=TOKEN_TILES))

@@ -367,7 +367,6 @@ def tile_multiheadattentionunit_pa_e_kernel(
         for r in range(TOKEN_TILES):
             pieces[after_0 + r, 0] = {1: [(norm_turn, 0, r)], 3: [(norm_sum, 0, r)]}
             pieces[after_0 + r, 1] = {1: [(norm_scale, 0, r), (norm_spread, 0, r)], 3: [(norm_finish, 0, r)]}
-        pieces[after_0 + 1, 0][1] = pieces[after_0, 1].pop(3) + pieces[after_0 + 1, 0][1]
         for n in range(len(steps)):
             for i in range(PAIR):
                 multiply_unit(n, i, pieces.get((n, i), {}))

@@ -67,7 +67,12 @@ def tile_multiheadattentionunit_pa_e_kernel(
 
         def load_attn(b, h):
             a_raw[b, h] = keep.tile([P, TOKEN_TILES, DV], BF16, name="a_raw%d_%d" % (b, h))
-            nc.sync.dma_start(out=a_raw[b, h][:], in_=attn[b, h].rearrange("(p r) k -> p r k", r=TOKEN_TILES))
+            loads = GROUPS if h == 0 else 1
+            for k in range(loads):
+                cols = slice(DV // loads * k, DV // loads * (k + 1))
+                nc.sync.dma_start(
+                    out=a_raw[b, h][:, :, cols], in_=attn[b, h].rearrange("(p r) k -> p r k", r=TOKEN_TILES)[:, :, cols]
+                )
 
         w_words = {}
 
@@ -184,7 +189,14 @@ def tile_multiheadattentionunit_pa_e_kernel(
             if i == 0:
                 a_codes[n] = stage.tile([P, PAIR, GROUPS, S], U32, name="a_codes", align_bytes=64)
                 a_scales[n] = stage.tile([P, PAIR, GROUPS, S], U8, name="a_scales", align_bytes=64)
-            if True:
+            if n == 0:
+                for g in range(GROUPS):
+                    nc.vector.quantize_mx(
+                        out=a_codes[n][:, i, g].bitcast(FP8X4),
+                        scales=a_scales[n][:, i, g],
+                        in_=grouped[n][:, i, g].rearrange("p n t -> p (n t)"),
+                    )
+            else:
                 nc.vector.quantize_mx(
                     out=a_codes[n][:, i].rearrange("p g n -> p (g n)").bitcast(FP8X4),
                     scales=a_scales[n][:, i].rearrange("p g n -> p (g n)"),
@@ -283,22 +295,27 @@ def tile_multiheadattentionunit_pa_e_kernel(
                         stop=(j == BANK // P - 1),
                     )
 
-        def norm_sum_seeded(b, r):
+        def norm_sum_seeded(b, r, share):
             x[b, r] = stage.tile([P, D], F32, name="x")
             neg_mean[b, r] = small.tile([P, 1], F32, name="neg_mean")
             half_sums = small.tile([P, D // BANK], F32)
             nc.scalar.activation(
                 out=x[b, r][:, 0:BANK], in_=x_t[b, r, 0][:], func=ACT.Identity, accum_out=half_sums[:, 0:1]
             )
-            nc.vector.tensor_scalar(
-                out=x[b, r][:, BANK : 2 * BANK],
-                in0=x_t[b, r, 1][:],
-                scalar1=1.0,
-                scalar2=None,
-                op0=ALU.mult,
-                op1=ALU.add,
-                accum_out=half_sums[:, 1:2],
-            )
+            if share:
+                nc.vector.tensor_scalar(
+                    out=x[b, r][:, BANK : 2 * BANK],
+                    in0=x_t[b, r, 1][:],
+                    scalar1=1.0,
+                    scalar2=None,
+                    op0=ALU.mult,
+                    op1=ALU.add,
+                    accum_out=half_sums[:, 1:2],
+                )
+            else:
+                nc.scalar.activation(
+                    out=x[b, r][:, BANK : 2 * BANK], in_=x_t[b, r, 1][:], func=ACT.Identity, accum_out=half_sums[:, 1:2]
+                )
             nc.vector.tensor_scalar(
                 out=neg_mean[b, r][:],
                 in0=half_sums[:, 0:1],
@@ -377,7 +394,7 @@ def tile_multiheadattentionunit_pa_e_kernel(
             norm_seed(B - 1, r)
         for r in range(TOKEN_TILES):
             norm_turn_onto(B - 1, r)
-            norm_sum_seeded(B - 1, r)
+            norm_sum_seeded(B - 1, r, r == 0)
             norm_scale(B - 1, r)
         for r in range(TOKEN_TILES):
             norm_spread(B - 1, r)

@@ -81,7 +81,7 @@ def tile_multiheadattentionunit_pa_e_kernel(
             width = D // loads
             w_words[h] = []
             for k in range(loads):
-                piece = keep.tile([P, GROUPS, width], U32, name="w_words%d_%d" % (h, k), align_bytes=64)
+                piece = keep.tile([P, GROUPS, width], U32, name="w_words%d_%d" % (h, k), align_bytes=256)
                 w_words[h].append(piece)
                 nc.sync.dma_start(
                     out=piece[:].bitcast(I32),
@@ -90,7 +90,7 @@ def tile_multiheadattentionunit_pa_e_kernel(
                     .bitcast(I32),
                 )
 
-        w_planes = keep.tile([P, PLANE_SETS, D], U8, align_bytes=64)
+        w_planes = keep.tile([P, PLANE_SETS, D], U8, align_bytes=256)
         nc.vector.memset(w_planes[:].bitcast(I32), 0)
 
         def load_planes(pair):
@@ -164,7 +164,7 @@ def tile_multiheadattentionunit_pa_e_kernel(
 
         def transpose_unit(n, i):
             if i == 0:
-                grouped[n] = stage.tile([P, PAIR, GROUPS, S, 4], BF16, name="grouped", align_bytes=64)
+                grouped[n] = stage.tile([P, PAIR, GROUPS, S, 4], BF16, name="grouped", align_bytes=256)
             unit = steps[n][i]
             if True:
                 for g in range(GROUPS):
@@ -187,8 +187,8 @@ def tile_multiheadattentionunit_pa_e_kernel(
 
         def quantise_unit(n, i):
             if i == 0:
-                a_codes[n] = stage.tile([P, PAIR, GROUPS, S], U32, name="a_codes", align_bytes=64)
-                a_scales[n] = stage.tile([P, PAIR, GROUPS, S], U8, name="a_scales", align_bytes=64)
+                a_codes[n] = stage.tile([P, PAIR, GROUPS, S], U32, name="a_codes", align_bytes=256)
+                a_scales[n] = stage.tile([P, PAIR, GROUPS, S], U8, name="a_scales", align_bytes=256)
             if n == 0:
                 for g in range(GROUPS):
                     nc.vector.quantize_mx(

@@ -58,8 +58,9 @@ def tile_multiheadattentionunit_pa_e_kernel(
         warm = keep.tile([P, 1], F32)
         nc.scalar.activation(out=warm[:], in_=one[:], func=ACT.Sqrt)
 
-        steps = [[(b, h) for b in range(B)] for h in range(PAIR)]
-        steps += [[(b, PAIR * pair + i) for i in range(PAIR)] for b in range(B) for pair in range(1, PAIRS)]
+        both = 3
+        order = [(b, h) for h in range(both) for b in range(B)] + [(b, h) for b in range(B) for h in range(both, H)]
+        steps = [order[k : k + PAIR] for k in range(0, len(order), PAIR)]
         def by_scalar(b, h, bank):
             return bank % 2 == 0 and not (bank > 0 and b == B - 1 and h in (0, H - 1))
 
@@ -100,30 +101,29 @@ def tile_multiheadattentionunit_pa_e_kernel(
                     in_=Wo_scales[PLANES * pair : PLANES * (pair + 1), 4 * quadrant : 4 * quadrant + 4, :].bitcast(I32),
                 )
 
-        for h in range(PAIR):
-            for unit in steps[h]:
-                load_attn(*unit)
-            if h == 0:
-                load_planes(0)
-            load_weight(h)
         q_sb = {}
         gamma_b = keep.tile([P, D], BF16)
         beta_b = keep.tile([P, D], BF16)
         for b in range(B):
             q_sb[b] = keep.tile([P, TOKEN_TILES, D], BF16, name="q_sb%d" % b)
-        for pair in range(1, PAIRS):
-            load_planes(pair)
-        for n in range(PAIR, len(steps)):
-            if n == len(steps) - 1:
+        order = [unit for step in steps for unit in step]
+        first_after_0 = 1 + max([k for k in range(len(order)) if order[k][0] == 0])
+        for unit in order[0:PAIR]:
+            load_attn(*unit)
+        load_planes(0)
+        load_weight(0)
+        for k in range(len(order)):
+            if k + PAIR < len(order):
+                load_attn(*order[k + PAIR])
+            if k + 1 < len(order) and order[k + 1][1] not in w_words:
+                load_weight(order[k + 1][1])
+                if order[k + 1][1] == 1:
+                    for pair in range(1, PAIRS):
+                        load_planes(pair)
+            if k + PAIR == first_after_0 + 1:
                 nc.sync.dma_start(out=q_sb[0][:], in_=query_inputs[0].rearrange("(p r) d -> p r d", r=TOKEN_TILES))
                 nc.sync.dma_start(out=gamma_b[:], in_=gamma.partition_broadcast(P))
                 nc.sync.dma_start(out=beta_b[:], in_=beta.partition_broadcast(P))
-            for unit in steps[n]:
-                load_attn(*unit)
-            b, h = steps[n][0]
-            if b == 0:
-                for i in range(PAIR):
-                    load_weight(h + i)
         nc.sync.dma_start(out=q_sb[1][:], in_=query_inputs[1].rearrange("(p r) d -> p r d", r=TOKEN_TILES))
 
         b_rows32 = keep.tile([P, P], F32)
@@ -379,11 +379,12 @@ def tile_multiheadattentionunit_pa_e_kernel(
             transpose_unit(0, i)
         for i in range(PAIR):
             quantise_unit(0, i)
-        after_0 = 1 + max([n for n in range(len(steps)) if steps[n][0][0] == 0])
         pieces = {}
         for r in range(TOKEN_TILES):
-            pieces[after_0 + r, 0] = {1: [(norm_turn, 0, r)], 3: [(norm_sum, 0, r)]}
-            pieces[after_0 + r, 1] = {1: [(norm_scale, 0, r), (norm_spread, 0, r)], 3: [(norm_finish, 0, r)]}
+            k = first_after_0 + PAIR * r
+            pieces[k // PAIR, k % PAIR] = {1: [(norm_turn, 0, r)], 3: [(norm_sum, 0, r)]}
+            k = k + 1
+            pieces[k // PAIR, k % PAIR] = {1: [(norm_scale, 0, r), (norm_spread, 0, r)], 3: [(norm_finish, 0, r)]}
         for n in range(len(steps)):
             for i in range(PAIR):
                 multiply_unit(n, i, pieces.get((n, i), {}))

@@ -78,7 +78,7 @@ def tile_multiheadattentionunit_pa_e_kernel(
         w_words = {}
 
         def load_weight(h):
-            loads = D_TILES // PER_BANK if h == 0 else 1
+            loads = D_TILES // PER_BANK if h == 0 else (2 if h == H - 1 else 1)
             width = D // loads
             w_words[h] = []
             for k in range(loads):
@@ -120,9 +120,10 @@ def tile_multiheadattentionunit_pa_e_kernel(
                 if order[k + 1][1] == 1:
                     for pair in range(1, PAIRS):
                         load_planes(pair)
-            if k + PAIR == first_after_0 + 1:
+            if k + PAIR == first_after_0 + 2:
                 nc.sync.dma_start(out=q_sb[0][:], in_=query_inputs[0].rearrange("(p r) d -> p r d", r=TOKEN_TILES))
                 nc.sync.dma_start(out=gamma_b[:], in_=gamma.partition_broadcast(P))
+            if k + PAIR == first_after_0 + 3:
                 nc.sync.dma_start(out=beta_b[:], in_=beta.partition_broadcast(P))
         nc.sync.dma_start(out=q_sb[1][:], in_=query_inputs[1].rearrange("(p r) d -> p r d", r=TOKEN_TILES))
 

from contextlib import ExitStack

import concourse.mybir as mybir
from concourse.masks import make_identity

F32 = mybir.dt.float32
BF16 = mybir.dt.bfloat16
I32 = mybir.dt.int32
U32 = mybir.dt.uint32
U8 = mybir.dt.uint8
FP8X4 = mybir.dt.float8_e4m3fn_x4
ALU = mybir.AluOpType
ACT = mybir.ActivationFunctionType

B, H, S, DV, D = 2, 8, 256, 1024, 1024
LN_EPS = 1e-3
FLOPS = 2 * B * H * S * DV * D

P = 128
K_PASS = 4 * P
GROUPS = DV // K_PASS
WORDS = K_PASS // 2
D_TILES = D // P
TOKEN_TILES = S // P
PAIR = 2
PAIRS = H // PAIR
BANK = 512
PER_BANK = BANK // S
PLANES = 4
PLANE_SETS = H * GROUPS // PLANES
assert PLANES == PAIR * GROUPS and PLANE_SETS == PAIRS


def tile_multiheadattentionunit_pa_e_kernel(
    tc, attn, Wo_words, Wo_scales, bo, query_inputs, gamma, beta, out
):
    nc = tc.nc
    with ExitStack() as ctx:
        ctx.enter_context(tc.manual_schedule())
        keep = ctx.enter_context(tc.tile_pool(name="keep", bufs=1))
        stage = ctx.enter_context(tc.tile_pool(name="stage", bufs=2))
        terms = ctx.enter_context(tc.tile_pool(name="terms", bufs=4))
        small = ctx.enter_context(tc.tile_pool(name="small", bufs=4))
        psum_t = ctx.enter_context(tc.psum_pool(name="psum_t", bufs=4))
        psum_mx = ctx.enter_context(tc.psum_pool(name="psum_mx", bufs=4))

        ident = keep.tile([P, P], F32)
        make_identity(nc, ident[:])
        ident_bf = keep.tile([P, P], BF16)
        make_identity(nc, ident_bf[:])

        b_rows = keep.tile([P, P], BF16)
        nc.sync.dma_start(out=b_rows[0 : H * D_TILES, :], in_=bo.rearrange("h (t p) -> (h t) p", p=P))
        nc.vector.memset(b_rows[H * D_TILES : P, :], 0.0)

        one = keep.tile([P, 1], F32)
        nc.vector.memset(one[:], 1.0)
        warm = keep.tile([P, 1], F32)
        nc.scalar.activation(out=warm[:], in_=one[:], func=ACT.Sqrt)

        both = 3
        order = [(b, h) for h in range(both) for b in range(B)] + [(b, h) for b in range(B) for h in range(both, H)]
        steps = [order[k : k + PAIR] for k in range(0, len(order), PAIR)]
        def by_scalar(b, h, bank):
            return bank % 2 == 0 and not (bank > 0 and b == B - 1 and h in (0, H - 1))

        a_raw = {}

        def load_attn(b, h):
            a_raw[b, h] = keep.tile([P, TOKEN_TILES, DV], BF16, name="a_raw%d_%d" % (b, h))
            loads = GROUPS if h == 0 else 1
            for k in range(loads):
                cols = slice(DV // loads * k, DV // loads * (k + 1))
                nc.sync.dma_start(
                    out=a_raw[b, h][:, :, cols], in_=attn[b, h].rearrange("(p r) k -> p r k", r=TOKEN_TILES)[:, :, cols]
                )

        w_words = {}

        def load_weight(h):
            loads = D_TILES // PER_BANK if h == 0 else (2 if h == H - 1 else 1)
            width = D // loads
            w_words[h] = []
            for k in range(loads):
                piece = keep.tile([P, GROUPS, width], U32, name="w_words%d_%d" % (h, k), align_bytes=256)
                w_words[h].append(piece)
                nc.sync.dma_start(
                    out=piece[:].bitcast(I32),
                    in_=Wo_words[GROUPS * h : GROUPS * (h + 1)]
                    .rearrange("g p n t -> p g (n t)")[:, :, 4 * width * k : 4 * width * (k + 1)]
                    .bitcast(I32),
                )

        w_planes = keep.tile([P, PLANE_SETS, D], U8, align_bytes=256)
        nc.vector.memset(w_planes[:].bitcast(I32), 0)

        def load_planes(pair):
            for quadrant in range(4):
                nc.sync.dma_start(
                    out=w_planes[32 * quadrant : 32 * quadrant + 4 * PLANES, pair, :].bitcast(I32),
                    in_=Wo_scales[PLANES * pair : PLANES * (pair + 1), 4 * quadrant : 4 * quadrant + 4, :].bitcast(I32),
                )

        q_sb = {}
        gamma_b = keep.tile([P, D], BF16)
        beta_b = keep.tile([P, D], BF16)
        for b in range(B):
            q_sb[b] = keep.tile([P, TOKEN_TILES, D], BF16, name="q_sb%d" % b)
        order = [unit for step in steps for unit in step]
        first_after_0 = 1 + max([k for k in range(len(order)) if order[k][0] == 0])
        for unit in order[0:PAIR]:
            load_attn(*unit)
        load_planes(0)
        load_weight(0)
        for k in range(len(order)):
            if k + PAIR < len(order):
                load_attn(*order[k + PAIR])
            if k + 1 < len(order) and order[k + 1][1] not in w_words:
                load_weight(order[k + 1][1])
                if order[k + 1][1] == 1:
                    for pair in range(1, PAIRS):
                        load_planes(pair)
            if k + PAIR == first_after_0 + 2:
                nc.sync.dma_start(out=q_sb[0][:], in_=query_inputs[0].rearrange("(p r) d -> p r d", r=TOKEN_TILES))
                nc.sync.dma_start(out=gamma_b[:], in_=gamma.partition_broadcast(P))
            if k + PAIR == first_after_0 + 3:
                nc.sync.dma_start(out=beta_b[:], in_=beta.partition_broadcast(P))
        nc.sync.dma_start(out=q_sb[1][:], in_=query_inputs[1].rearrange("(p r) d -> p r d", r=TOKEN_TILES))

        b_rows32 = keep.tile([P, P], F32)
        nc.vector.tensor_copy(out=b_rows32[:], in_=b_rows[:])
        b_cols = psum_t.tile([P, P], F32, tag="t")
        nc.tensor.transpose(b_cols[:], b_rows32[:], ident[:])
        bias = keep.tile([P, H, D_TILES], F32)
        neg_bias = keep.tile([P, H, D_TILES], F32)
        bias_sum = {}
        nc.vector.tensor_copy(out=bias[:].rearrange("p h t -> p (h t)"), in_=b_cols[:, 0 : H * D_TILES])
        nc.vector.tensor_scalar(
            out=neg_bias[:].rearrange("p h t -> p (h t)"),
            in0=b_cols[:, 0 : H * D_TILES],
            scalar1=-1.0,
            scalar2=None,
            op0=ALU.mult,
        )
        for b in range(B):
            bias_sum[b] = keep.tile([P, D_TILES], F32, name="bias_sum%d" % b)
            nc.vector.tensor_reduce(
                out=bias_sum[b][:], in_=bias[:].rearrange("p h t -> p t h"), axis=mybir.AxisListType.X, op=ALU.add
            )
            for bank in range(D_TILES // PER_BANK):
                heads = [h for h in range(H) if not by_scalar(b, h, bank)]
                if 0 < len(heads) < H:
                    assert len(heads) == 2
                    d_tiles = slice(PER_BANK * bank, PER_BANK * (bank + 1))
                    nc.vector.tensor_tensor(
                        out=bias_sum[b][:, d_tiles], in0=bias[:, heads[0], d_tiles], in1=bias[:, heads[1], d_tiles], op=ALU.add
                    )

        grouped = {}
        a_codes = {}
        a_scales = {}
        head_sum = {}
        for b in range(B):
            head_sum[b] = keep.tile([P, D_TILES, S], F32, name="head_sum%d" % b)

        def transpose_unit(n, i):
            if i == 0:
                grouped[n] = stage.tile([P, PAIR, GROUPS, S, 4], BF16, name="grouped", align_bytes=256)
            unit = steps[n][i]
            if True:
                for g in range(GROUPS):
                    pairs_t = psum_t.tile([P, 2, S], F32, tag="t")
                    for u in range(2):
                        for r in range(TOKEN_TILES):
                            words = a_raw[unit][:, r, :].bitcast(F32)
                            nc.tensor.transpose(
                                pairs_t[:, u, P * r : P * (r + 1)],
                                words[:, WORDS * g + u : WORDS * (g + 1) : 2],
                                ident[:],
                            )
                    nc.scalar.copy(
                        out=grouped[n][:, i, g]
                        .rearrange("p n t -> p (n t)")
                        .bitcast(F32)
                        .rearrange("p (n u) -> p n u", u=2),
                        in_=pairs_t[:].rearrange("p u n -> p n u"),
                    )

        def quantise_unit(n, i):
            if i == 0:
                a_codes[n] = stage.tile([P, PAIR, GROUPS, S], U32, name="a_codes", align_bytes=256)
                a_scales[n] = stage.tile([P, PAIR, GROUPS, S], U8, name="a_scales", align_bytes=256)
            if n == 0:
                for g in range(GROUPS):
                    nc.vector.quantize_mx(
                        out=a_codes[n][:, i, g].bitcast(FP8X4),
                        scales=a_scales[n][:, i, g],
                        in_=grouped[n][:, i, g].rearrange("p n t -> p (n t)"),
                    )
            else:
                nc.vector.quantize_mx(
                    out=a_codes[n][:, i].rearrange("p g n -> p (g n)").bitcast(FP8X4),
                    scales=a_scales[n][:, i].rearrange("p g n -> p (g n)"),
                    in_=grouped[n][:, i].rearrange("p g n t -> p (g n t)"),
                )

        def leave_psum(b, h, first_t, products):
            total = head_sum[b][:, first_t : first_t + PER_BANK, :]
            if by_scalar(b, h, first_t // PER_BANK):
                term = total if h == 0 else terms.tile([P, PER_BANK, S], F32, name="term")[:]
                for j in range(PER_BANK):
                    t = first_t + j
                    nc.scalar.activation(
                        out=term[:, j, :], in_=products[:, j, :], func=ACT.Relu, bias=bias[:, h, t : t + 1]
                    )
                if h > 0:
                    nc.gpsimd.tensor_tensor(out=total, in0=total, in1=term, op=ALU.add)
            else:
                for j in range(PER_BANK):
                    t = first_t + j
                    if h == 0:
                        nc.vector.tensor_scalar(
                            out=total[:, j, :],
                            in0=products[:, j, :],
                            scalar1=neg_bias[:, h, t : t + 1],
                            scalar2=bias_sum[b][:, t : t + 1],
                            op0=ALU.max,
                            op1=ALU.add,
                        )
                    else:
                        nc.vector.scalar_tensor_tensor(
                            out=total[:, j, :],
                            in0=products[:, j, :],
                            scalar=neg_bias[:, h, t : t + 1],
                            in1=total[:, j, :],
                            op0=ALU.max,
                            op1=ALU.add,
                        )

        def multiply_unit(n, i, behind_bank):
            b, h = steps[n][i]
            for first_t in range(0, D_TILES, PER_BANK):
                products = psum_mx.tile([P, PER_BANK, S], F32)
                for j in range(PER_BANK):
                    t = first_t + j
                    for g in range(GROUPS):
                        plane_set, plane = divmod(GROUPS * h + g, PLANES)
                        k, t_in_piece = divmod(t, D_TILES // len(w_words[h]))
                        nc.tensor.matmul_mx(
                            out=products[:, j, :],
                            lhsT=w_words[h][k][:, g, P * t_in_piece : P * (t_in_piece + 1)].bitcast(FP8X4),
                            lhsT_scale=w_planes[4 * plane : P, plane_set, P * t : P * (t + 1)],
                            rhs=a_codes[n][:, i, g, :].bitcast(FP8X4),
                            rhs_scale=a_scales[n][:, i, g, :],
                            start=(g == 0),
                            stop=(g == GROUPS - 1),
                        )
                leave_psum(b, h, first_t, products[:])
                for piece in behind_bank.get(first_t // PER_BANK, []):
                    piece[0](*piece[1:])

        x_t = {}
        x = {}
        y = {}
        neg_mean = {}
        std = {}

        def norm_turn(b, r):
            for c in range(D // BANK):
                bank = psum_t.tile([P, BANK], F32, tag="t")
                x_t[b, r, c] = bank
                for j in range(BANK // P):
                    nc.tensor.transpose(
                        bank[:, P * j : P * (j + 1)],
                        head_sum[b][:, (BANK // P) * c + j, P * r : P * (r + 1)],
                        ident[:],
                    )

        def norm_seed(b, r):
            for c in range(D // BANK):
                bank = psum_t.tile([P, BANK], F32, tag="t")
                x_t[b, r, c] = bank
                nc.tensor.matmul(
                    bank[:], lhsT=ident_bf[:], rhs=q_sb[b][:, r, BANK * c : BANK * (c + 1)], start=True, stop=False
                )

        def norm_turn_onto(b, r):
            for c in range(D // BANK):
                for j in range(BANK // P):
                    nc.tensor.matmul(
                        x_t[b, r, c][:, P * j : P * (j + 1)],
                        lhsT=head_sum[b][:, (BANK // P) * c + j, P * r : P * (r + 1)],
                        rhs=ident[:],
                        is_transpose=True,
                        start=False,
                        stop=(j == BANK // P - 1),
                    )

        def norm_sum_seeded(b, r, share):
            x[b, r] = stage.tile([P, D], F32, name="x")
            neg_mean[b, r] = small.tile([P, 1], F32, name="neg_mean")
            half_sums = small.tile([P, D // BANK], F32)
            nc.scalar.activation(
                out=x[b, r][:, 0:BANK], in_=x_t[b, r, 0][:], func=ACT.Identity, accum_out=half_sums[:, 0:1]
            )
            if share:
                nc.vector.tensor_scalar(
                    out=x[b, r][:, BANK : 2 * BANK],
                    in0=x_t[b, r, 1][:],
                    scalar1=1.0,
                    scalar2=None,
                    op0=ALU.mult,
                    op1=ALU.add,
                    accum_out=half_sums[:, 1:2],
                )
            else:
                nc.scalar.activation(
                    out=x[b, r][:, BANK : 2 * BANK], in_=x_t[b, r, 1][:], func=ACT.Identity, accum_out=half_sums[:, 1:2]
                )
            nc.vector.tensor_scalar(
                out=neg_mean[b, r][:],
                in0=half_sums[:, 0:1],
                scalar1=half_sums[:, 1:2],
                scalar2=-1.0 / D,
                op0=ALU.add,
                op1=ALU.mult,
            )

        def norm_sum(b, r):
            x[b, r] = stage.tile([P, D], F32, name="x")
            neg_mean[b, r] = small.tile([P, 1], F32, name="neg_mean")
            half_sums = small.tile([P, D // BANK], F32)
            for c in range(D // BANK):
                nc.vector.scalar_tensor_tensor(
                    out=x[b, r][:, BANK * c : BANK * (c + 1)],
                    in0=x_t[b, r, c][:],
                    scalar=1.0,
                    in1=q_sb[b][:, r, BANK * c : BANK * (c + 1)],
                    op0=ALU.mult,
                    op1=ALU.add,
                    accum_out=half_sums[:, c : c + 1],
                )
            nc.vector.tensor_scalar(
                out=neg_mean[b, r][:],
                in0=half_sums[:, 0:1],
                scalar1=half_sums[:, 1:2],
                scalar2=-1.0 / D,
                op0=ALU.add,
                op1=ALU.mult,
            )

        def norm_scale(b, r):
            y[b, r] = stage.tile([P, D], F32, name="y")
            nc.vector.scalar_tensor_tensor(
                out=y[b, r][:], in0=x[b, r][:], scalar=neg_mean[b, r][:], in1=gamma_b[:], op0=ALU.add, op1=ALU.mult
            )

        def norm_spread(b, r):
            squares = stage.tile([P, D], BF16)
            sum_sq = small.tile([P, 1], F32)
            std[b, r] = small.tile([P, 1], F32, name="std")
            nc.scalar.activation(
                out=squares[:], in_=x[b, r][:], func=ACT.Square, bias=neg_mean[b, r][:], accum_out=sum_sq[:]
            )
            nc.scalar.activation(out=std[b, r][:], in_=sum_sq[:], func=ACT.Sqrt, bias=LN_EPS, scale=1.0 / D)

        def norm_finish(b, r, pieces=1):
            rstd = small.tile([P, 1], F32)
            nc.vector.reciprocal(out=rstd[:], in_=std[b, r][:])
            for piece in range(pieces):
                cols = slice(D // pieces * piece, D // pieces * (piece + 1))
                nc.vector.scalar_tensor_tensor(
                    out=y[b, r][:, cols], in0=y[b, r][:, cols], scalar=rstd[:], in1=beta_b[:, cols], op0=ALU.mult, op1=ALU.add
                )
                nc.sync.dma_start(
                    out=out[b].rearrange("(p r) d -> p r d", r=TOKEN_TILES)[:, r, cols], in_=y[b, r][:, cols]
                )

        for i in range(PAIR):
            transpose_unit(0, i)
        for i in range(PAIR):
            quantise_unit(0, i)
        pieces = {}
        for r in range(TOKEN_TILES):
            k = first_after_0 + PAIR * r
            pieces[k // PAIR, k % PAIR] = {1: [(norm_turn, 0, r)], 3: [(norm_sum, 0, r)]}
            k = k + 1
            pieces[k // PAIR, k % PAIR] = {1: [(norm_scale, 0, r), (norm_spread, 0, r)], 3: [(norm_finish, 0, r)]}
        for n in range(len(steps)):
            for i in range(PAIR):
                multiply_unit(n, i, pieces.get((n, i), {}))
                if n + 1 < len(steps):
                    transpose_unit(n + 1, i)
                    quantise_unit(n + 1, i)
        for r in range(TOKEN_TILES):
            norm_seed(B - 1, r)
        for r in range(TOKEN_TILES):
            norm_turn_onto(B - 1, r)
            norm_sum_seeded(B - 1, r, r == 0)
            norm_scale(B - 1, r)
        for r in range(TOKEN_TILES):
            norm_spread(B - 1, r)
            norm_finish(B - 1, r, 2 * (r + 1))
